import numpy as np
import ml_dtypes


def mxq(x, axis, fmt="e4m3"):
    dtype, down = {"e4m3": (ml_dtypes.float8_e4m3fn, 7), "e5m2": (ml_dtypes.float8_e5m2, 14)}[fmt]
    v = np.moveaxis(np.asarray(x, np.float32).astype(ml_dtypes.bfloat16).astype(np.float64), axis, -1)
    blocks = v.reshape(v.shape[:-1] + (-1, 32))
    amax = np.abs(blocks).max(-1, keepdims=True)
    byte = np.maximum(np.where(amax > 0, np.frexp(amax)[1] - 1 + 127, 0) - down, 1)
    scale = np.exp2(byte - 127.0)
    codes = (blocks / scale).astype(np.float32).astype(dtype).astype(np.float64)
    return np.moveaxis((codes * scale).reshape(v.shape), -1, axis)


BF16 = ml_dtypes.bfloat16


def bf(x):
    return np.asarray(x, np.float32).astype(BF16)


def f64(x):
    return np.asarray(x).astype(np.float64)


B, N, SHOT, D = 16384, 128, 5, 512
C = 2.0


def setup_inputs():
    g = np.random.standard_normal(D) * C
    x1 = (g + np.random.standard_normal((B, D))) / np.sqrt(D)
    x2 = (g + np.random.standard_normal((N, SHOT, D)) * np.sqrt(SHOT)) / np.sqrt(D)
    return {"x1": bf(x1.reshape(B, D, 1, 1)), "x2": bf(x2.reshape(N, SHOT, D, 1, 1))}


def reference(x1, x2):
    x1, x2 = f64(x1), f64(x2)
    b = x1.shape[0]
    q = x1.reshape(b, -1)
    n = x2.shape[0]
    protos = x2.reshape(n, x2.shape[1], -1).mean(axis=1)
    q_sq = np.sum(q * q, axis=-1, keepdims=True)
    p_sq = np.sum(protos * protos, axis=-1)
    cross = mxq(q, 1, "e4m3") @ mxq(protos, 1, "e4m3").T
    score = -(q_sq - 2.0 * cross + p_sq[None, :])
    return score

@@ -1,0 +1,224 @@
+from contextlib import ExitStack
+
+import concourse.mybir as mybir
+from concourse.masks import make_identity
+
+F32 = mybir.dt.float32
+BF16 = mybir.dt.bfloat16
+U32 = mybir.dt.uint32
+U8 = mybir.dt.uint8
+FP8X4 = mybir.dt.float8_e4m3fn_x4
+ALU = mybir.AluOpType
+ACT = mybir.ActivationFunctionType
+
+P = 128
+B = 16384
+N = 128
+SHOT = 5
+D = 512
+W = D // 2
+FLOPS = 2 * B * N * D
+
+SIZES = (2, 2, 4, 4) + (8,) * 14 + (2, 2)
+assert sum(SIZES) * P == B
+FIRST_LOADS = 7
+
+
+def tile_proto_metric_t_kernel(tc, x1, x2, out):
+    nc = tc.nc
+    q_rows = x1.rearrange("b d x y -> b (d x y)")
+    shots = x2.rearrange("n s d x y -> n (s d x y)")
+    n_batches = len(SIZES)
+    first = [sum(SIZES[:s]) for s in range(n_batches)]
+
+    with ExitStack() as ctx:
+        const = ctx.enter_context(tc.tile_pool(name="const", bufs=1))
+        grp_pool = ctx.enter_context(tc.tile_pool(name="grp", bufs=3))
+        code_pool = ctx.enter_context(tc.tile_pool(name="code", bufs=4))
+        junk_pool = ctx.enter_context(tc.tile_pool(name="junk", bufs=4))
+        o_pool = ctx.enter_context(tc.tile_pool(name="o", bufs=4))
+        ps_t = ctx.enter_context(tc.psum_pool(name="ps_t", bufs=4))
+        ps_m = ctx.enter_context(tc.psum_pool(name="ps_m", bufs=4))
+        ctx.enter_context(tc.manual_schedule())
+
+        x_sb = {}
+        banks = {}
+        grouped = {}
+        codes = {}
+        planes = {}
+        q_sq = {}
+        cross = {}
+        loaded = [0]
+
+        def load(s):
+            t = SIZES[s]
+            x_t = const.tile([P, t * D], BF16, name="x%d" % s)
+            rows = q_rows[first[s] * P : (first[s] + t) * P, :]
+            nc.sync.dma_start(out=x_t[:], in_=rows.rearrange("(p t) d -> p (t d)", t=t))
+            x_sb[s] = x_t
+            loaded[0] = s + 1
+
+        def transposes(s):
+            words = x_sb[s][:].bitcast(F32)
+            banks[s] = []
+            for h in range(SIZES[s] // 2):
+                bank = ps_t.tile([P, 4 * P], F32, name="xt", tag="xt")
+                for k in range(4):
+                    nc.tensor.transpose(
+                        out=bank[:, k * P : (k + 1) * P],
+                        in_=words[:, (4 * h + k) * P : (4 * h + k + 1) * P],
+                        identity=ident_f[:],
+                    )
+                banks[s].append(bank)
+
+        def evacuate(s, h):
+            if h == 0:
+                g_t = grp_pool.tile([P, SIZES[s] * D], BF16, name="grp", tag="grp", align_bytes=64)
+                grouped[s] = g_t
+            dst = grouped[s][:].bitcast(F32)[:, h * 4 * P : (h + 1) * 4 * P]
+            nc.vector.tensor_copy(
+                out=dst.rearrange("p (a i u) -> p a i u", a=2, u=2),
+                in_=banks[s][h][:].rearrange("p (a u i) -> p a i u", a=2, u=2),
+            )
+
+        def quantise(s):
+            c_t = code_pool.tile([P, SIZES[s] * P], U32, name="codes", tag="codes", align_bytes=64)
+            s_t = code_pool.tile([P, SIZES[s] * P], U8, name="plane", tag="plane", align_bytes=64)
+            nc.vector.quantize_mx(out=c_t[:].bitcast(FP8X4), scales=s_t[:], in_=grouped[s][:])
+            codes[s] = c_t
+            planes[s] = s_t
+
+        def multiply(s):
+            cross[s] = []
+            for a in range(SIZES[s]):
+                if a % 4 == 0:
+                    acc = ps_m.tile([P, 4 * N], F32, name="acc", tag="acc")
+                    cross[s].append(acc)
+                nc.tensor.matmul_mx(
+                    out=cross[s][a // 4][:, (a % 4) * N : (a % 4 + 1) * N],
+                    lhsT=codes[s][:, a * P : (a + 1) * P].bitcast(FP8X4),
+                    lhsT_scale=planes[s][:, a * P : (a + 1) * P],
+                    rhs=p_codes[:].bitcast(FP8X4),
+                    rhs_scale=p_plane[:],
+                    start=True,
+                    stop=True,
+                )
+
+        def squares(s, a0, a1):
+            if a0 == 0:
+                n_t = const.tile([P, SIZES[s]], F32, name="qsq%d" % s)
+                q_sq[s] = n_t
+            for a in range(a0, a1):
+                junk = junk_pool.tile([P, D], BF16, name="junk", tag="junk")
+                nc.scalar.activation(
+                    out=junk[:],
+                    in_=x_sb[s][:, a * D : (a + 1) * D],
+                    func=ACT.Square,
+                    accum_out=q_sq[s][:, a : a + 1],
+                )
+
+        def finish(s):
+            t = SIZES[s]
+            o_t = o_pool.tile([P, t * N], F32, name="o", tag="o")
+            for a in range(t):
+                nc.vector.scalar_tensor_tensor(
+                    out=o_t[:, a * N : (a + 1) * N],
+                    in0=cross[s][a // 4][:, (a % 4) * N : (a % 4 + 1) * N],
+                    scalar=q_sq[s][:, a : a + 1],
+                    in1=p_sq[:],
+                    op0=ALU.subtract,
+                    op1=ALU.subtract,
+                )
+            rows = out[first[s] * P : (first[s] + t) * P, :]
+            nc.sync.dma_start(out=rows.rearrange("(p t) j -> p (t j)", t=t), in_=o_t[:])
+            if loaded[0] < n_batches:
+                load(loaded[0])
+
+        load(0)
+        load(1)
+        load(2)
+        x2_sb = const.tile([P, SHOT * D], BF16, name="x2_sb")
+        nc.sync.dma_start(out=x2_sb[:], in_=shots)
+        for s in range(3, FIRST_LOADS):
+            load(s)
+        ident_f = const.tile([P, P], F32, name="ident_f")
+        make_identity(nc, ident_f[:])
+        ident_b = const.tile([P, P], BF16, name="ident_b")
+        make_identity(nc, ident_b[:])
+        ones = const.tile([P, P], F32, name="ones")
+        nc.vector.memset(ones[:], 1.0)
+
+        transposes(0)
+        squares(0, 0, 2)
+        evacuate(0, 0)
+        transposes(1)
+        squares(1, 0, 2)
+        evacuate(1, 0)
+        quantise(0)
+        transposes(2)
+        squares(2, 0, 4)
+        evacuate(2, 0)
+        evacuate(2, 1)
+        quantise(1)
+        quantise(2)
+
+        sums = ps_m.tile([P, 4 * N], F32, name="sums", tag="acc")
+        x2_v = x2_sb[:].rearrange("n (s u p e) -> n s u e p", s=SHOT, u=2, e=2)
+        for t4 in range(4):
+            for s in range(SHOT):
+                nc.tensor.matmul(
+                    out=sums[:, t4 * N : (t4 + 1) * N],
+                    lhsT=x2_v[:, s, t4 // 2, t4 % 2, :],
+                    rhs=ident_b[:],
+                    start=(s == 0),
+                    stop=(s == SHOT - 1),
+                )
+        transposes(3)
+        squares(3, 0, 2)
+        p_grp = const.tile([P, 4 * N], BF16, name="p_grp", align_bytes=64)
+        nc.vector.tensor_scalar_mul(
+            out=p_grp[:].rearrange("p (n t) -> p n t", t=4),
+            in0=sums[:].rearrange("p (t n) -> p n t", t=4),
+            scalar1=2.0 / SHOT,
+        )
+        p_sqr = const.tile([P, 4 * N], F32, name="p_sqr")
+        nc.scalar.activation(out=p_sqr[:], in_=sums[:], func=ACT.Square, scale=1.0 / SHOT)
+        squares(3, 2, 4)
+        evacuate(3, 0)
+        p_codes = const.tile([P, N], U32, name="p_codes", align_bytes=64)
+        p_plane = const.tile([P, N], U8, name="p_plane", align_bytes=64)
+        nc.vector.quantize_mx(out=p_codes[:].bitcast(FP8X4), scales=p_plane[:], in_=p_grp[:])
+        evacuate(3, 1)
+        quantise(3)
+        norms = ps_m.tile([P, N], F32, name="norms", tag="acc")
+        for t4 in range(4):
+            nc.tensor.matmul(
+                out=norms[:],
+                lhsT=ones[:],
+                rhs=p_sqr[:, t4 * N : (t4 + 1) * N],
+                start=(t4 == 0),
+                stop=(t4 == 3),
+            )
+        p_sq = const.tile([P, N], F32, name="p_sq")
+        nc.vector.tensor_copy(out=p_sq[:], in_=norms[:])
+        multiply(0)
+        multiply(1)
+        multiply(2)
+        transposes(4)
+        squares(4, 0, SIZES[4])
+        multiply(3)
+        finish(0)
+        finish(1)
+        finish(2)
+
+        for s in range(4, n_batches + 1):
+            if s < n_batches:
+                for h in range(SIZES[s] // 2):
+                    evacuate(s, h)
+            if s + 1 < n_batches:
+                transposes(s + 1)
+                squares(s + 1, 0, SIZES[s + 1])
+            finish(s - 1)
+            if s < n_batches:
+                quantise(s)
+                multiply(s)

@@ -22,6 +22,8 @@ FLOPS = 2 * B * N * D
 SIZES = (2, 2, 4, 4) + (8,) * 14 + (2, 2)
 assert sum(SIZES) * P == B
 FIRST_LOADS = 7
+G_TILES = 2
+AX = mybir.AxisListType
 
 
 def tile_proto_metric_t_kernel(tc, x1, x2, out):
@@ -38,7 +40,9 @@ def tile_proto_metric_t_kernel(tc, x1, x2, out):
         junk_pool = ctx.enter_context(tc.tile_pool(name="junk", bufs=4))
         o_pool = ctx.enter_context(tc.tile_pool(name="o", bufs=4))
         ps_t = ctx.enter_context(tc.psum_pool(name="ps_t", bufs=4))
-        ps_m = ctx.enter_context(tc.psum_pool(name="ps_m", bufs=4))
+        ps_m = ctx.enter_context(tc.psum_pool(name="ps_m", bufs=3))
+        ps_r = ctx.enter_context(tc.psum_pool(name="ps_r", bufs=1))
+        sq_pool = ctx.enter_context(tc.tile_pool(name="sq", bufs=2))
         ctx.enter_context(tc.manual_schedule())
 
         x_sb = {}
@@ -48,7 +52,13 @@ def tile_proto_metric_t_kernel(tc, x1, x2, out):
         planes = {}
         q_sq = {}
         cross = {}
+        sq_t = {}
+        r_bank = {}
+        q_sq_g = {}
         loaded = [0]
+
+        def g_tiles(s):
+            return G_TILES if SIZES[s] == 8 else 0
 
         def load(s):
             t = SIZES[s]
@@ -76,10 +86,48 @@ def tile_proto_metric_t_kernel(tc, x1, x2, out):
                 g_t = grp_pool.tile([P, SIZES[s] * D], BF16, name="grp", tag="grp", align_bytes=64)
                 grouped[s] = g_t
             dst = grouped[s][:].bitcast(F32)[:, h * 4 * P : (h + 1) * 4 * P]
-            nc.vector.tensor_copy(
-                out=dst.rearrange("p (a i u) -> p a i u", a=2, u=2),
-                in_=banks[s][h][:].rearrange("p (a u i) -> p a i u", a=2, u=2),
+            if SIZES[s] == 8 and h == 3:
+                nc.scalar.copy(
+                    out=dst.rearrange("p (a i u) -> p a i u", a=2, u=2),
+                    in_=banks[s][h][:].rearrange("p (a u i) -> p a i u", a=2, u=2),
+                )
+            else:
+                nc.vector.tensor_copy(
+                    out=dst.rearrange("p (a i u) -> p a i u", a=2, u=2),
+                    in_=banks[s][h][:].rearrange("p (a u i) -> p a i u", a=2, u=2),
+                )
+
+        def g_squares(s):
+            g = g_tiles(s)
+            sq = sq_pool.tile([P, g * D], F32, name="sq", tag="sq")
+            src = grouped[s][:, 0 : g * D].rearrange("p (a i t) -> p a t i", a=g, t=4)
+            nc.gpsimd.tensor_tensor(
+                out=sq[:].rearrange("p (a t i) -> p a t i", a=g, t=4), in0=src, in1=src, op=ALU.mult
             )
+            sq_t[s] = sq
+
+        def g_sums(s):
+            g = g_tiles(s)
+            r_t = ps_r.tile([P, g * P], F32, name="r", tag="r")
+            for a in range(g):
+                for t4 in range(4):
+                    nc.tensor.matmul(
+                        out=r_t[:, a * P : (a + 1) * P],
+                        lhsT=sq_t[s][:, (4 * a + t4) * P : (4 * a + t4 + 1) * P],
+                        rhs=ident_f[:],
+                        start=(t4 == 0),
+                        stop=(t4 == 3),
+                        is_transpose=True,
+                    )
+            r_bank[s] = r_t
+
+        def g_reduce(s):
+            g = g_tiles(s)
+            n_g = const.tile([P, g], F32, name="qsg%d" % s)
+            nc.vector.tensor_reduce(
+                out=n_g[:], in_=r_bank[s][:].rearrange("p (a k) -> p a k", a=g), axis=AX.X, op=ALU.add
+            )
+            q_sq_g[s] = n_g
 
         def quantise(s):
             c_t = code_pool.tile([P, SIZES[s] * P], U32, name="codes", tag="codes", align_bytes=64)
@@ -105,7 +153,7 @@ def tile_proto_metric_t_kernel(tc, x1, x2, out):
                 )
 
         def squares(s, a0, a1):
-            if a0 == 0:
+            if s not in q_sq:
                 n_t = const.tile([P, SIZES[s]], F32, name="qsq%d" % s)
                 q_sq[s] = n_t
             for a in range(a0, a1):
@@ -124,7 +172,7 @@ def tile_proto_metric_t_kernel(tc, x1, x2, out):
                 nc.vector.scalar_tensor_tensor(
                     out=o_t[:, a * N : (a + 1) * N],
                     in0=cross[s][a // 4][:, (a % 4) * N : (a % 4 + 1) * N],
-                    scalar=q_sq[s][:, a : a + 1],
+                    scalar=(q_sq_g[s][:, a : a + 1] if a < g_tiles(s) else q_sq[s][:, a : a + 1]),
                     in1=p_sq[:],
                     op0=ALU.subtract,
                     op1=ALU.subtract,
@@ -205,9 +253,9 @@ def tile_proto_metric_t_kernel(tc, x1, x2, out):
         multiply(1)
         multiply(2)
         transposes(4)
-        squares(4, 0, SIZES[4])
-        multiply(3)
+        squares(4, g_tiles(4), SIZES[4])
         finish(0)
+        multiply(3)
         finish(1)
         finish(2)
 
@@ -215,10 +263,16 @@ def tile_proto_metric_t_kernel(tc, x1, x2, out):
             if s < n_batches:
                 for h in range(SIZES[s] // 2):
                     evacuate(s, h)
+                    if h == 0 and g_tiles(s):
+                        g_squares(s)
             if s + 1 < n_batches:
                 transposes(s + 1)
-                squares(s + 1, 0, SIZES[s + 1])
+                squares(s + 1, g_tiles(s + 1), SIZES[s + 1])
+            if g_tiles(s - 1):
+                g_reduce(s - 1)
             finish(s - 1)
             if s < n_batches:
+                if g_tiles(s):
+                    g_sums(s)
                 quantise(s)
                 multiply(s)

@@ -19,11 +19,11 @@ D = 512
 W = D // 2
 FLOPS = 2 * B * N * D
 
-SIZES = (2, 2, 4, 4) + (8,) * 14 + (2, 2)
+SIZES = (2, 2, 4, 4) + (8,) * 14 + (4,)
+S_EVAC = (5, 7, 9, 11, 13, 15, 17)
+AX = mybir.AxisListType
 assert sum(SIZES) * P == B
 FIRST_LOADS = 7
-G_TILES = 2
-AX = mybir.AxisListType
 
 
 def tile_proto_metric_t_kernel(tc, x1, x2, out):
@@ -41,8 +41,8 @@ def tile_proto_metric_t_kernel(tc, x1, x2, out):
         o_pool = ctx.enter_context(tc.tile_pool(name="o", bufs=4))
         ps_t = ctx.enter_context(tc.psum_pool(name="ps_t", bufs=4))
         ps_m = ctx.enter_context(tc.psum_pool(name="ps_m", bufs=3))
-        ps_r = ctx.enter_context(tc.psum_pool(name="ps_r", bufs=1))
-        sq_pool = ctx.enter_context(tc.tile_pool(name="sq", bufs=2))
+        ps_j = ctx.enter_context(tc.psum_pool(name="ps_j", bufs=1))
+        sq_pool = ctx.enter_context(tc.tile_pool(name="sq", bufs=1))
         ctx.enter_context(tc.manual_schedule())
 
         x_sb = {}
@@ -52,13 +52,24 @@ def tile_proto_metric_t_kernel(tc, x1, x2, out):
         planes = {}
         q_sq = {}
         cross = {}
-        sq_t = {}
-        r_bank = {}
         q_sq_g = {}
+        tree = {}
         loaded = [0]
 
         def g_tiles(s):
-            return G_TILES if SIZES[s] == 8 else 0
+            return 1 if SIZES[s] == 8 else 0
+
+        def g_squares(s):
+            sq = sq_pool.tile([P, D], F32, name="sq", tag="sq")
+            nc.gpsimd.tensor_tensor(out=sq[:], in0=x_sb[s][:, 0:D], in1=x_sb[s][:, 0:D], op=ALU.mult)
+            nc.gpsimd.tensor_tensor(out=sq[:, 0:256], in0=sq[:, 0:256], in1=sq[:, 256:512], op=ALU.add)
+            nc.gpsimd.tensor_tensor(out=sq[:, 0:128], in0=sq[:, 0:128], in1=sq[:, 128:256], op=ALU.add)
+            tree[s] = sq
+
+        def g_reduce(s):
+            n_g = const.tile([P, 1], F32, name="qsg%d" % s)
+            nc.vector.tensor_reduce(out=n_g[:], in_=tree[s][:, 0:128], axis=AX.X, op=ALU.add)
+            q_sq_g[s] = n_g
 
         def load(s):
             t = SIZES[s]
@@ -68,10 +79,22 @@ def tile_proto_metric_t_kernel(tc, x1, x2, out):
             x_sb[s] = x_t
             loaded[0] = s + 1
 
-        def transposes(s):
+        def idle_pass(s):
+            nc.tensor.matmul_mx(
+                out=waste[:],
+                lhsT=p_codes[:].bitcast(FP8X4),
+                lhsT_scale=p_plane[:],
+                rhs=codes[s][:, 0 : 4 * P].bitcast(FP8X4),
+                rhs_scale=planes[s][:, 0 : 4 * P],
+                start=True,
+                stop=True,
+            )
+
+        def transposes(s, h0=0, h1=None):
             words = x_sb[s][:].bitcast(F32)
-            banks[s] = []
-            for h in range(SIZES[s] // 2):
+            if h0 == 0:
+                banks[s] = []
+            for h in range(h0, SIZES[s] // 2 if h1 is None else h1):
                 bank = ps_t.tile([P, 4 * P], F32, name="xt", tag="xt")
                 for k in range(4):
                     nc.tensor.transpose(
@@ -86,7 +109,7 @@ def tile_proto_metric_t_kernel(tc, x1, x2, out):
                 g_t = grp_pool.tile([P, SIZES[s] * D], BF16, name="grp", tag="grp", align_bytes=64)
                 grouped[s] = g_t
             dst = grouped[s][:].bitcast(F32)[:, h * 4 * P : (h + 1) * 4 * P]
-            if SIZES[s] == 8 and h == 3:
+            if h == 3 and s in S_EVAC:
                 nc.scalar.copy(
                     out=dst.rearrange("p (a i u) -> p a i u", a=2, u=2),
                     in_=banks[s][h][:].rearrange("p (a u i) -> p a i u", a=2, u=2),
@@ -96,38 +119,6 @@ def tile_proto_metric_t_kernel(tc, x1, x2, out):
                     out=dst.rearrange("p (a i u) -> p a i u", a=2, u=2),
                     in_=banks[s][h][:].rearrange("p (a u i) -> p a i u", a=2, u=2),
                 )
-
-        def g_squares(s):
-            g = g_tiles(s)
-            sq = sq_pool.tile([P, g * D], F32, name="sq", tag="sq")
-            src = grouped[s][:, 0 : g * D].rearrange("p (a i t) -> p a t i", a=g, t=4)
-            nc.gpsimd.tensor_tensor(
-                out=sq[:].rearrange("p (a t i) -> p a t i", a=g, t=4), in0=src, in1=src, op=ALU.mult
-            )
-            sq_t[s] = sq
-
-        def g_sums(s):
-            g = g_tiles(s)
-            r_t = ps_r.tile([P, g * P], F32, name="r", tag="r")
-            for a in range(g):
-                for t4 in range(4):
-                    nc.tensor.matmul(
-                        out=r_t[:, a * P : (a + 1) * P],
-                        lhsT=sq_t[s][:, (4 * a + t4) * P : (4 * a + t4 + 1) * P],
-                        rhs=ident_f[:],
-                        start=(t4 == 0),
-                        stop=(t4 == 3),
-                        is_transpose=True,
-                    )
-            r_bank[s] = r_t
-
-        def g_reduce(s):
-            g = g_tiles(s)
-            n_g = const.tile([P, g], F32, name="qsg%d" % s)
-            nc.vector.tensor_reduce(
-                out=n_g[:], in_=r_bank[s][:].rearrange("p (a k) -> p a k", a=g), axis=AX.X, op=ALU.add
-            )
-            q_sq_g[s] = n_g
 
         def quantise(s):
             c_t = code_pool.tile([P, SIZES[s] * P], U32, name="codes", tag="codes", align_bytes=64)
@@ -249,30 +240,38 @@ def tile_proto_metric_t_kernel(tc, x1, x2, out):
             )
         p_sq = const.tile([P, N], F32, name="p_sq")
         nc.vector.tensor_copy(out=p_sq[:], in_=norms[:])
+        waste = ps_j.tile([P, 4 * N], F32, name="waste")
         multiply(0)
         multiply(1)
         multiply(2)
         transposes(4)
         squares(4, g_tiles(4), SIZES[4])
+        g_squares(4)
         finish(0)
         multiply(3)
         finish(1)
         finish(2)
 
-        for s in range(4, n_batches + 1):
-            if s < n_batches:
-                for h in range(SIZES[s] // 2):
-                    evacuate(s, h)
-                    if h == 0 and g_tiles(s):
-                        g_squares(s)
-            if s + 1 < n_batches:
-                transposes(s + 1)
-                squares(s + 1, g_tiles(s + 1), SIZES[s + 1])
-            if g_tiles(s - 1):
-                g_reduce(s - 1)
+        last = n_batches - 1
+        for s in range(4, last):
+            g_reduce(s)
+            if g_tiles(s + 1):
+                g_squares(s + 1)
+            for h in range(SIZES[s] // 2):
+                evacuate(s, h)
+            half = SIZES[s + 1] // 4
+            transposes(s + 1, 0, half)
+            if s > 4:
+                idle_pass(s - 1)
+            transposes(s + 1, half, None)
+            squares(s + 1, g_tiles(s + 1), SIZES[s + 1])
             finish(s - 1)
-            if s < n_batches:
-                if g_tiles(s):
-                    g_sums(s)
-                quantise(s)
-                multiply(s)
+            quantise(s)
+            multiply(s)
+            idle_pass(s)
+        for h in range(SIZES[last] // 2):
+            evacuate(last, h)
+        quantise(last)
+        multiply(last)
+        finish(last - 1)
+        finish(last)

@@ -20,8 +20,7 @@ W = D // 2
 FLOPS = 2 * B * N * D
 
 SIZES = (2, 2, 4, 4) + (8,) * 14 + (4,)
-S_EVAC = (5, 7, 9, 11, 13, 15, 17)
-AX = mybir.AxisListType
+S_EVAC = (5, 7, 8, 9, 11, 12, 13, 15, 17)
 assert sum(SIZES) * P == B
 FIRST_LOADS = 7
 
@@ -42,7 +41,7 @@ def tile_proto_metric_t_kernel(tc, x1, x2, out):
         ps_t = ctx.enter_context(tc.psum_pool(name="ps_t", bufs=4))
         ps_m = ctx.enter_context(tc.psum_pool(name="ps_m", bufs=3))
         ps_j = ctx.enter_context(tc.psum_pool(name="ps_j", bufs=1))
-        sq_pool = ctx.enter_context(tc.tile_pool(name="sq", bufs=1))
+        sq_pool = ctx.enter_context(tc.tile_pool(name="sq", bufs=4))
         ctx.enter_context(tc.manual_schedule())
 
         x_sb = {}
@@ -52,24 +51,36 @@ def tile_proto_metric_t_kernel(tc, x1, x2, out):
         planes = {}
         q_sq = {}
         cross = {}
+        sums_g = {}
         q_sq_g = {}
-        tree = {}
         loaded = [0]
 
         def g_tiles(s):
-            return 1 if SIZES[s] == 8 else 0
+            return 1 + s % 2 if SIZES[s] == 8 and s < n_batches - 2 else 0
 
         def g_squares(s):
-            sq = sq_pool.tile([P, D], F32, name="sq", tag="sq")
-            nc.gpsimd.tensor_tensor(out=sq[:], in0=x_sb[s][:, 0:D], in1=x_sb[s][:, 0:D], op=ALU.mult)
-            nc.gpsimd.tensor_tensor(out=sq[:, 0:256], in0=sq[:, 0:256], in1=sq[:, 256:512], op=ALU.add)
-            nc.gpsimd.tensor_tensor(out=sq[:, 0:128], in0=sq[:, 0:128], in1=sq[:, 128:256], op=ALU.add)
-            tree[s] = sq
+            sums_g[s] = []
+            for a in range(g_tiles(s)):
+                sq = sq_pool.tile([P, D], F32, name="sq", tag="sq")
+                half = sq_pool.tile([P, D // 2], F32, name="half", tag="half")
+                quarter = sq_pool.tile([P, D // 4], F32, name="quarter", tag="quarter")
+                x_t = grouped[s][:, a * D : (a + 1) * D]
+                nc.gpsimd.tensor_tensor(out=sq[:], in0=x_t, in1=x_t, op=ALU.mult)
+                v4 = sq[:].rearrange("p (i t) -> p i t", t=4)
+                nc.gpsimd.tensor_tensor(
+                    out=half[:].rearrange("p (i t) -> p i t", t=2), in0=v4[:, :, 0:2], in1=v4[:, :, 2:4], op=ALU.add
+                )
+                v2 = half[:].rearrange("p (i t) -> p i t", t=2)
+                nc.gpsimd.tensor_tensor(out=quarter[:], in0=v2[:, :, 0], in1=v2[:, :, 1], op=ALU.add)
+                sums_g[s].append(quarter)
 
-        def g_reduce(s):
-            n_g = const.tile([P, 1], F32, name="qsg%d" % s)
-            nc.vector.tensor_reduce(out=n_g[:], in_=tree[s][:, 0:128], axis=AX.X, op=ALU.add)
-            q_sq_g[s] = n_g
+        def g_sum(s):
+            cols = ps_j.tile([P, 4 * N], F32, name="cols", tag="cols")
+            for a in range(g_tiles(s)):
+                nc.tensor.matmul(
+                    out=cols[:, a : a + 1], lhsT=sums_g[s][a][:], rhs=ones[:, 0:1], start=True, stop=True
+                )
+            q_sq_g[s] = cols
 
         def load(s):
             t = SIZES[s]
@@ -78,17 +89,6 @@ def tile_proto_metric_t_kernel(tc, x1, x2, out):
             nc.sync.dma_start(out=x_t[:], in_=rows.rearrange("(p t) d -> p (t d)", t=t))
             x_sb[s] = x_t
             loaded[0] = s + 1
-
-        def idle_pass(s):
-            nc.tensor.matmul_mx(
-                out=waste[:],
-                lhsT=p_codes[:].bitcast(FP8X4),
-                lhsT_scale=p_plane[:],
-                rhs=codes[s][:, 0 : 4 * P].bitcast(FP8X4),
-                rhs_scale=planes[s][:, 0 : 4 * P],
-                start=True,
-                stop=True,
-            )
 
         def transposes(s, h0=0, h1=None):
             words = x_sb[s][:].bitcast(F32)
@@ -159,11 +159,12 @@ def tile_proto_metric_t_kernel(tc, x1, x2, out):
         def finish(s):
             t = SIZES[s]
             o_t = o_pool.tile([P, t * N], F32, name="o", tag="o")
-            for a in range(t):
+            g = g_tiles(s)
+            for a in list(range(g, t)) + list(range(g)):
                 nc.vector.scalar_tensor_tensor(
                     out=o_t[:, a * N : (a + 1) * N],
                     in0=cross[s][a // 4][:, (a % 4) * N : (a % 4 + 1) * N],
-                    scalar=(q_sq_g[s][:, a : a + 1] if a < g_tiles(s) else q_sq[s][:, a : a + 1]),
+                    scalar=(q_sq_g[s][:, a : a + 1] if a < g else q_sq[s][:, a : a + 1]),
                     in1=p_sq[:],
                     op0=ALU.subtract,
                     op1=ALU.subtract,
@@ -240,13 +241,11 @@ def tile_proto_metric_t_kernel(tc, x1, x2, out):
             )
         p_sq = const.tile([P, N], F32, name="p_sq")
         nc.vector.tensor_copy(out=p_sq[:], in_=norms[:])
-        waste = ps_j.tile([P, 4 * N], F32, name="waste")
         multiply(0)
         multiply(1)
         multiply(2)
         transposes(4)
         squares(4, g_tiles(4), SIZES[4])
-        g_squares(4)
         finish(0)
         multiply(3)
         finish(1)
@@ -254,23 +253,22 @@ def tile_proto_metric_t_kernel(tc, x1, x2, out):
 
         last = n_batches - 1
         for s in range(4, last):
-            g_reduce(s)
-            if g_tiles(s + 1):
-                g_squares(s + 1)
             for h in range(SIZES[s] // 2):
                 evacuate(s, h)
+                if h == 0:
+                    g_squares(s)
             half = SIZES[s + 1] // 4
             transposes(s + 1, 0, half)
             if s > 4:
-                idle_pass(s - 1)
+                g_sum(s - 1)
             transposes(s + 1, half, None)
             squares(s + 1, g_tiles(s + 1), SIZES[s + 1])
             finish(s - 1)
             quantise(s)
             multiply(s)
-            idle_pass(s)
         for h in range(SIZES[last] // 2):
             evacuate(last, h)
+        g_sum(last - 1)
         quantise(last)
         multiply(last)
         finish(last - 1)

@@ -20,7 +20,7 @@ W = D // 2
 FLOPS = 2 * B * N * D
 
 SIZES = (2, 2, 4, 4) + (8,) * 14 + (4,)
-S_EVAC = (5, 7, 8, 9, 11, 12, 13, 15, 17)
+S_EVAC = (5, 8, 11, 14)
 assert sum(SIZES) * P == B
 FIRST_LOADS = 7
 
@@ -56,7 +56,7 @@ def tile_proto_metric_t_kernel(tc, x1, x2, out):
         loaded = [0]
 
         def g_tiles(s):
-            return 1 + s % 2 if SIZES[s] == 8 and s < n_batches - 2 else 0
+            return 1 if SIZES[s] == 8 and s < n_batches - 2 else 0
 
         def g_squares(s):
             sums_g[s] = []
@@ -109,7 +109,7 @@ def tile_proto_metric_t_kernel(tc, x1, x2, out):
                 g_t = grp_pool.tile([P, SIZES[s] * D], BF16, name="grp", tag="grp", align_bytes=64)
                 grouped[s] = g_t
             dst = grouped[s][:].bitcast(F32)[:, h * 4 * P : (h + 1) * 4 * P]
-            if h == 3 and s in S_EVAC:
+            if (h == 3 and s in S_EVAC) or s == n_batches - 1:
                 nc.scalar.copy(
                     out=dst.rearrange("p (a i u) -> p a i u", a=2, u=2),
                     in_=banks[s][h][:].rearrange("p (a u i) -> p a i u", a=2, u=2),

@@ -20,7 +20,7 @@ W = D // 2
 FLOPS = 2 * B * N * D
 
 SIZES = (2, 2, 4, 4) + (8,) * 14 + (4,)
-S_EVAC = (5, 8, 11, 14)
+S_EVAC = (4, 5, 7, 8, 10, 11, 13, 14, 16, 17)
 assert sum(SIZES) * P == B
 FIRST_LOADS = 7
 

@@ -20,7 +20,8 @@ W = D // 2
 FLOPS = 2 * B * N * D
 
 SIZES = (2, 2, 4, 4) + (8,) * 14 + (4,)
-S_EVAC = (4, 5, 7, 8, 10, 11, 13, 14, 16, 17)
+S_EVAC = (5, 7, 9, 11, 13, 15, 17)
+GRAM = (6, 8, 10, 12, 14, 16)
 assert sum(SIZES) * P == B
 FIRST_LOADS = 7
 
@@ -74,11 +75,34 @@ def tile_proto_metric_t_kernel(tc, x1, x2, out):
                 nc.gpsimd.tensor_tensor(out=quarter[:], in0=v2[:, :, 0], in1=v2[:, :, 1], op=ALU.add)
                 sums_g[s].append(quarter)
 
+        def gram_tile(s):
+            return g_tiles(s) if s in GRAM else None
+
+        def gram_diagonal(s):
+            junk = junk_pool.tile([P, N], F32, name="junk_g", tag="junk_g")
+            a = gram_tile(s)
+            nc.vector.scalar_tensor_tensor(
+                out=junk[:],
+                in0=q_sq_g[s][:, 0:P],
+                scalar=1.0,
+                in1=ident_f[:],
+                op0=ALU.mult,
+                op1=ALU.mult,
+                accum_out=q_sq[s][:, a : a + 1],
+            )
+
         def g_sum(s):
             cols = ps_j.tile([P, 4 * N], F32, name="cols", tag="cols")
+            if s in GRAM:
+                a = gram_tile(s)
+                g4 = grouped[s][:, a * D : (a + 1) * D].rearrange("p (i t) -> p t i", t=4)
+                for k in range(4):
+                    nc.tensor.matmul(
+                        out=cols[:, 0:P], lhsT=g4[:, k, :], rhs=g4[:, k, :], start=(k == 0), stop=(k == 3)
+                    )
             for a in range(g_tiles(s)):
                 nc.tensor.matmul(
-                    out=cols[:, a : a + 1], lhsT=sums_g[s][a][:], rhs=ones[:, 0:1], start=True, stop=True
+                    out=cols[:, P + a : P + a + 1], lhsT=sums_g[s][a][:], rhs=ones[:, 0:1], start=True, stop=True
                 )
             q_sq_g[s] = cols
 
@@ -160,11 +184,12 @@ def tile_proto_metric_t_kernel(tc, x1, x2, out):
             t = SIZES[s]
             o_t = o_pool.tile([P, t * N], F32, name="o", tag="o")
             g = g_tiles(s)
-            for a in list(range(g, t)) + list(range(g)):
+            last_ones = list(range(g)) + ([gram_tile(s)] if s in GRAM else [])
+            for a in [a for a in range(t) if a not in last_ones] + last_ones:
                 nc.vector.scalar_tensor_tensor(
                     out=o_t[:, a * N : (a + 1) * N],
                     in0=cross[s][a // 4][:, (a % 4) * N : (a % 4 + 1) * N],
-                    scalar=(q_sq_g[s][:, a : a + 1] if a < g else q_sq[s][:, a : a + 1]),
+                    scalar=(q_sq_g[s][:, P + a : P + a + 1] if a < g else q_sq[s][:, a : a + 1]),
                     in1=p_sq[:],
                     op0=ALU.subtract,
                     op1=ALU.subtract,
@@ -262,13 +287,16 @@ def tile_proto_metric_t_kernel(tc, x1, x2, out):
             if s > 4:
                 g_sum(s - 1)
             transposes(s + 1, half, None)
-            squares(s + 1, g_tiles(s + 1), SIZES[s + 1])
+            squares(s + 1, g_tiles(s + 1) + (s + 1 in GRAM), SIZES[s + 1])
+            if s - 1 in GRAM:
+                gram_diagonal(s - 1)
             finish(s - 1)
             quantise(s)
             multiply(s)
         for h in range(SIZES[last] // 2):
             evacuate(last, h)
-        g_sum(last - 1)
+        if g_tiles(last - 1):
+            g_sum(last - 1)
         quantise(last)
         multiply(last)
         finish(last - 1)

@@ -151,10 +151,26 @@ def tile_proto_metric_t_kernel(tc, x1, x2, out):
             codes[s] = c_t
             planes[s] = s_t
 
-        def multiply(s):
+        def keep_warm(s):
             cross[s] = []
+            for b in range(SIZES[s] // 4):
+                acc = ps_m.tile([P, 4 * N], F32, name="acc", tag="acc")
+                cross[s].append(acc)
+                nc.tensor.matmul_mx(
+                    out=acc[:],
+                    lhsT=p_codes[:].bitcast(FP8X4),
+                    lhsT_scale=p_plane[:],
+                    rhs=codes[s - 1][:, 0 : 4 * P].bitcast(FP8X4),
+                    rhs_scale=planes[s - 1][:, 0 : 4 * P],
+                    start=True,
+                    stop=True,
+                )
+
+        def multiply(s):
+            if s not in cross:
+                cross[s] = []
             for a in range(SIZES[s]):
-                if a % 4 == 0:
+                if a % 4 == 0 and len(cross[s]) <= a // 4:
                     acc = ps_m.tile([P, 4 * N], F32, name="acc", tag="acc")
                     cross[s].append(acc)
                 nc.tensor.matmul_mx(
@@ -184,8 +200,7 @@ def tile_proto_metric_t_kernel(tc, x1, x2, out):
             t = SIZES[s]
             o_t = o_pool.tile([P, t * N], F32, name="o", tag="o")
             g = g_tiles(s)
-            last_ones = list(range(g)) + ([gram_tile(s)] if s in GRAM else [])
-            for a in [a for a in range(t) if a not in last_ones] + last_ones:
+            for a in ([2, 0, 1] + list(range(3, t)) if g else range(t)):
                 nc.vector.scalar_tensor_tensor(
                     out=o_t[:, a * N : (a + 1) * N],
                     in0=cross[s][a // 4][:, (a % 4) * N : (a % 4 + 1) * N],
@@ -282,11 +297,11 @@ def tile_proto_metric_t_kernel(tc, x1, x2, out):
                 evacuate(s, h)
                 if h == 0:
                     g_squares(s)
-            half = SIZES[s + 1] // 4
-            transposes(s + 1, 0, half)
-            if s > 4:
-                g_sum(s - 1)
-            transposes(s + 1, half, None)
+            transposes(s + 1)
+            if s not in GRAM:
+                keep_warm(s)
+            if g_tiles(s):
+                g_sum(s)
             squares(s + 1, g_tiles(s + 1) + (s + 1 in GRAM), SIZES[s + 1])
             if s - 1 in GRAM:
                 gram_diagonal(s - 1)
@@ -295,8 +310,6 @@ def tile_proto_metric_t_kernel(tc, x1, x2, out):
             multiply(s)
         for h in range(SIZES[last] // 2):
             evacuate(last, h)
-        if g_tiles(last - 1):
-            g_sum(last - 1)
         quantise(last)
         multiply(last)
         finish(last - 1)

@@ -151,13 +151,13 @@ def tile_proto_metric_t_kernel(tc, x1, x2, out):
             codes[s] = c_t
             planes[s] = s_t
 
-        def keep_warm(s):
-            cross[s] = []
-            for b in range(SIZES[s] // 4):
+        def keep_warm(s, passes):
+            if s not in cross:
                 acc = ps_m.tile([P, 4 * N], F32, name="acc", tag="acc")
-                cross[s].append(acc)
+                cross[s] = [acc]
+            for b in range(passes):
                 nc.tensor.matmul_mx(
-                    out=acc[:],
+                    out=cross[s][0][:],
                     lhsT=p_codes[:].bitcast(FP8X4),
                     lhsT_scale=p_plane[:],
                     rhs=codes[s - 1][:, 0 : 4 * P].bitcast(FP8X4),
@@ -297,9 +297,11 @@ def tile_proto_metric_t_kernel(tc, x1, x2, out):
                 evacuate(s, h)
                 if h == 0:
                     g_squares(s)
-            transposes(s + 1)
-            if s not in GRAM:
-                keep_warm(s)
+            half = SIZES[s + 1] // 4
+            transposes(s + 1, 0, half)
+            keep_warm(s, 2)
+            transposes(s + 1, half, None)
+            keep_warm(s, 1 if s in GRAM else 2)
             if g_tiles(s):
                 g_sum(s)
             squares(s + 1, g_tiles(s + 1) + (s + 1 in GRAM), SIZES[s + 1])

@@ -20,7 +20,7 @@ W = D // 2
 FLOPS = 2 * B * N * D
 
 SIZES = (2, 2, 4, 4) + (8,) * 14 + (4,)
-S_EVAC = (5, 7, 9, 11, 13, 15, 17)
+S_EVAC = (5, 6, 8, 9, 10, 12, 13, 14, 15, 16, 17)
 GRAM = (6, 8, 10, 12, 14, 16)
 assert sum(SIZES) * P == B
 FIRST_LOADS = 7

@@ -20,8 +20,7 @@ W = D // 2
 FLOPS = 2 * B * N * D
 
 SIZES = (2, 2, 4, 4) + (8,) * 14 + (4,)
-S_EVAC = (5, 6, 8, 9, 10, 12, 13, 14, 15, 16, 17)
-GRAM = (6, 8, 10, 12, 14, 16)
+GRAM = range(5, 17)
 assert sum(SIZES) * P == B
 FIRST_LOADS = 7
 
@@ -36,7 +35,7 @@ def tile_proto_metric_t_kernel(tc, x1, x2, out):
     with ExitStack() as ctx:
         const = ctx.enter_context(tc.tile_pool(name="const", bufs=1))
         grp_pool = ctx.enter_context(tc.tile_pool(name="grp", bufs=3))
-        code_pool = ctx.enter_context(tc.tile_pool(name="code", bufs=4))
+        code_pool = ctx.enter_context(tc.tile_pool(name="code", bufs=6))
         junk_pool = ctx.enter_context(tc.tile_pool(name="junk", bufs=4))
         o_pool = ctx.enter_context(tc.tile_pool(name="o", bufs=4))
         ps_t = ctx.enter_context(tc.psum_pool(name="ps_t", bufs=4))
@@ -57,7 +56,7 @@ def tile_proto_metric_t_kernel(tc, x1, x2, out):
         loaded = [0]
 
         def g_tiles(s):
-            return 1 if SIZES[s] == 8 and s < n_batches - 2 else 0
+            return 1 if s in GRAM else 0
 
         def g_squares(s):
             sums_g[s] = []
@@ -133,7 +132,7 @@ def tile_proto_metric_t_kernel(tc, x1, x2, out):
                 g_t = grp_pool.tile([P, SIZES[s] * D], BF16, name="grp", tag="grp", align_bytes=64)
                 grouped[s] = g_t
             dst = grouped[s][:].bitcast(F32)[:, h * 4 * P : (h + 1) * 4 * P]
-            if (h == 3 and s in S_EVAC) or s == n_batches - 1:
+            if h == 3 or s == n_batches - 1:
                 nc.scalar.copy(
                     out=dst.rearrange("p (a i u) -> p a i u", a=2, u=2),
                     in_=banks[s][h][:].rearrange("p (a u i) -> p a i u", a=2, u=2),
@@ -223,10 +222,15 @@ def tile_proto_metric_t_kernel(tc, x1, x2, out):
             load(s)
         ident_f = const.tile([P, P], F32, name="ident_f")
         make_identity(nc, ident_f[:])
-        ident_b = const.tile([P, P], BF16, name="ident_b")
-        make_identity(nc, ident_b[:])
         ones = const.tile([P, P], F32, name="ones")
         nc.vector.memset(ones[:], 1.0)
+
+        x2_sum = const.tile([P, D], F32, name="x2_sum")
+        nc.gpsimd.tensor_tensor(out=x2_sum[:], in0=x2_sb[:, 0:D], in1=x2_sb[:, D : 2 * D], op=ALU.add)
+        for s in range(2, SHOT):
+            nc.gpsimd.tensor_tensor(
+                out=x2_sum[:], in0=x2_sum[:], in1=x2_sb[:, s * D : (s + 1) * D], op=ALU.add
+            )
 
         transposes(0)
         squares(0, 0, 2)
@@ -241,58 +245,60 @@ def tile_proto_metric_t_kernel(tc, x1, x2, out):
         evacuate(2, 1)
         quantise(1)
         quantise(2)
+        transposes(3)
+        squares(3, 0, 4)
+        evacuate(3, 0)
+        evacuate(3, 1)
+        quantise(3)
+        transposes(4)
+        squares(4, g_tiles(4), 4)
 
         sums = ps_m.tile([P, 4 * N], F32, name="sums", tag="acc")
-        x2_v = x2_sb[:].rearrange("n (s u p e) -> n s u e p", s=SHOT, u=2, e=2)
         for t4 in range(4):
-            for s in range(SHOT):
-                nc.tensor.matmul(
-                    out=sums[:, t4 * N : (t4 + 1) * N],
-                    lhsT=x2_v[:, s, t4 // 2, t4 % 2, :],
-                    rhs=ident_b[:],
-                    start=(s == 0),
-                    stop=(s == SHOT - 1),
-                )
-        transposes(3)
-        squares(3, 0, 2)
+            c0 = 256 * (t4 // 2)
+            nc.tensor.transpose(
+                out=sums[:, t4 * N : (t4 + 1) * N],
+                in_=x2_sum[:, c0 + t4 % 2 : c0 + 256 : 2],
+                identity=ident_f[:],
+            )
+        for h in range(4):
+            evacuate(4, h)
         p_grp = const.tile([P, 4 * N], BF16, name="p_grp", align_bytes=64)
         nc.vector.tensor_scalar_mul(
             out=p_grp[:].rearrange("p (n t) -> p n t", t=4),
             in0=sums[:].rearrange("p (t n) -> p n t", t=4),
             scalar1=2.0 / SHOT,
         )
-        p_sqr = const.tile([P, 4 * N], F32, name="p_sqr")
-        nc.scalar.activation(out=p_sqr[:], in_=sums[:], func=ACT.Square, scale=1.0 / SHOT)
-        squares(3, 2, 4)
-        evacuate(3, 0)
+        p_junk = const.tile([P, D], BF16, name="p_junk")
+        p_norm = const.tile([P, 1], F32, name="p_norm")
+        nc.scalar.activation(
+            out=p_junk[:], in_=x2_sum[:], func=ACT.Square, scale=1.0 / SHOT, accum_out=p_norm[:]
+        )
+        squares(4, 4, 8)
+        norms = ps_m.tile([P, N], F32, name="norms", tag="acc")
+        nc.tensor.matmul(
+            out=norms[:], lhsT=p_norm[:].to_broadcast([P, P]), rhs=ident_f[:], start=True, stop=True
+        )
+        quantise(4)
         p_codes = const.tile([P, N], U32, name="p_codes", align_bytes=64)
         p_plane = const.tile([P, N], U8, name="p_plane", align_bytes=64)
         nc.vector.quantize_mx(out=p_codes[:].bitcast(FP8X4), scales=p_plane[:], in_=p_grp[:])
-        evacuate(3, 1)
-        quantise(3)
-        norms = ps_m.tile([P, N], F32, name="norms", tag="acc")
-        for t4 in range(4):
-            nc.tensor.matmul(
-                out=norms[:],
-                lhsT=ones[:],
-                rhs=p_sqr[:, t4 * N : (t4 + 1) * N],
-                start=(t4 == 0),
-                stop=(t4 == 3),
-            )
         p_sq = const.tile([P, N], F32, name="p_sq")
         nc.vector.tensor_copy(out=p_sq[:], in_=norms[:])
+        transposes(5)
+        squares(5, g_tiles(5) + (5 in GRAM), SIZES[5])
         multiply(0)
         multiply(1)
         multiply(2)
-        transposes(4)
-        squares(4, g_tiles(4), SIZES[4])
         finish(0)
         multiply(3)
         finish(1)
         finish(2)
+        multiply(4)
+        finish(3)
 
         last = n_batches - 1
-        for s in range(4, last):
+        for s in range(5, last):
             for h in range(SIZES[s] // 2):
                 evacuate(s, h)
                 if h == 0:
@@ -301,7 +307,7 @@ def tile_proto_metric_t_kernel(tc, x1, x2, out):
             transposes(s + 1, 0, half)
             keep_warm(s, 2)
             transposes(s + 1, half, None)
-            keep_warm(s, 1 if s in GRAM else 2)
+            keep_warm(s, 1)
             if g_tiles(s):
                 g_sum(s)
             squares(s + 1, g_tiles(s + 1) + (s + 1 in GRAM), SIZES[s + 1])

@@ -22,7 +22,7 @@ FLOPS = 2 * B * N * D
 SIZES = (2, 2, 4, 4) + (8,) * 14 + (4,)
 GRAM = range(5, 17)
 assert sum(SIZES) * P == B
-FIRST_LOADS = 7
+FIRST_LOADS = 9
 
 
 def tile_proto_metric_t_kernel(tc, x1, x2, out):
@@ -132,7 +132,7 @@ def tile_proto_metric_t_kernel(tc, x1, x2, out):
                 g_t = grp_pool.tile([P, SIZES[s] * D], BF16, name="grp", tag="grp", align_bytes=64)
                 grouped[s] = g_t
             dst = grouped[s][:].bitcast(F32)[:, h * 4 * P : (h + 1) * 4 * P]
-            if h == 3 or s == n_batches - 1:
+            if (h == 3 and s > 5) or (h == 2 and s == n_batches - 2) or s == n_batches - 1:
                 nc.scalar.copy(
                     out=dst.rearrange("p (a i u) -> p a i u", a=2, u=2),
                     in_=banks[s][h][:].rearrange("p (a u i) -> p a i u", a=2, u=2),
@@ -213,12 +213,11 @@ def tile_proto_metric_t_kernel(tc, x1, x2, out):
             if loaded[0] < n_batches:
                 load(loaded[0])
 
-        load(0)
-        load(1)
-        load(2)
+        for s in range(4):
+            load(s)
         x2_sb = const.tile([P, SHOT * D], BF16, name="x2_sb")
         nc.sync.dma_start(out=x2_sb[:], in_=shots)
-        for s in range(3, FIRST_LOADS):
+        for s in range(4, FIRST_LOADS):
             load(s)
         ident_f = const.tile([P, P], F32, name="ident_f")
         make_identity(nc, ident_f[:])
@@ -241,17 +240,20 @@ def tile_proto_metric_t_kernel(tc, x1, x2, out):
         quantise(0)
         transposes(2)
         squares(2, 0, 4)
+        quantise(1)
         evacuate(2, 0)
         evacuate(2, 1)
-        quantise(1)
-        quantise(2)
         transposes(3)
         squares(3, 0, 4)
+        quantise(2)
         evacuate(3, 0)
         evacuate(3, 1)
-        quantise(3)
         transposes(4)
-        squares(4, g_tiles(4), 4)
+        quantise(3)
+        for h in range(4):
+            evacuate(4, h)
+        squares(4, 0, 5)
+        transposes(5)
 
         sums = ps_m.tile([P, 4 * N], F32, name="sums", tag="acc")
         for t4 in range(4):
@@ -261,32 +263,36 @@ def tile_proto_metric_t_kernel(tc, x1, x2, out):
                 in_=x2_sum[:, c0 + t4 % 2 : c0 + 256 : 2],
                 identity=ident_f[:],
             )
+        p_junk = const.tile([P, D], BF16, name="p_junk")
+        p_norm = const.tile([P, 1], F32, name="p_norm")
+        nc.scalar.activation(
+            out=p_junk[:], in_=x2_sum[:], func=ACT.Square, scale=1.0 / SHOT, accum_out=p_norm[:]
+        )
         for h in range(4):
-            evacuate(4, h)
+            evacuate(5, h)
+            if h == 0:
+                g_squares(5)
+        squares(4, 5, 8)
+        norms = ps_m.tile([P, N], F32, name="norms", tag="acc")
+        nc.tensor.matmul(
+            out=norms[:], lhsT=p_norm[:].to_broadcast([P, P]), rhs=ident_f[:], start=True, stop=True
+        )
+        transposes(6)
         p_grp = const.tile([P, 4 * N], BF16, name="p_grp", align_bytes=64)
         nc.vector.tensor_scalar_mul(
             out=p_grp[:].rearrange("p (n t) -> p n t", t=4),
             in0=sums[:].rearrange("p (t n) -> p n t", t=4),
             scalar1=2.0 / SHOT,
         )
-        p_junk = const.tile([P, D], BF16, name="p_junk")
-        p_norm = const.tile([P, 1], F32, name="p_norm")
-        nc.scalar.activation(
-            out=p_junk[:], in_=x2_sum[:], func=ACT.Square, scale=1.0 / SHOT, accum_out=p_norm[:]
-        )
-        squares(4, 4, 8)
-        norms = ps_m.tile([P, N], F32, name="norms", tag="acc")
-        nc.tensor.matmul(
-            out=norms[:], lhsT=p_norm[:].to_broadcast([P, P]), rhs=ident_f[:], start=True, stop=True
-        )
         quantise(4)
         p_codes = const.tile([P, N], U32, name="p_codes", align_bytes=64)
         p_plane = const.tile([P, N], U8, name="p_plane", align_bytes=64)
         nc.vector.quantize_mx(out=p_codes[:].bitcast(FP8X4), scales=p_plane[:], in_=p_grp[:])
+        quantise(5)
         p_sq = const.tile([P, N], F32, name="p_sq")
         nc.vector.tensor_copy(out=p_sq[:], in_=norms[:])
-        transposes(5)
-        squares(5, g_tiles(5) + (5 in GRAM), SIZES[5])
+        for s in (5, 6):
+            squares(s, g_tiles(s) + (s in GRAM), SIZES[s])
         multiply(0)
         multiply(1)
         multiply(2)
@@ -296,9 +302,12 @@ def tile_proto_metric_t_kernel(tc, x1, x2, out):
         finish(2)
         multiply(4)
         finish(3)
+        g_sum(5)
+        multiply(5)
+        finish(4)
 
         last = n_batches - 1
-        for s in range(5, last):
+        for s in range(6, last):
             for h in range(SIZES[s] // 2):
                 evacuate(s, h)
                 if h == 0:
@@ -310,7 +319,8 @@ def tile_proto_metric_t_kernel(tc, x1, x2, out):
             keep_warm(s, 1)
             if g_tiles(s):
                 g_sum(s)
-            squares(s + 1, g_tiles(s + 1) + (s + 1 in GRAM), SIZES[s + 1])
+            if s < last - 1:
+                squares(s + 1, g_tiles(s + 1) + (s + 1 in GRAM), SIZES[s + 1])
             if s - 1 in GRAM:
                 gram_diagonal(s - 1)
             finish(s - 1)
@@ -318,6 +328,7 @@ def tile_proto_metric_t_kernel(tc, x1, x2, out):
             multiply(s)
         for h in range(SIZES[last] // 2):
             evacuate(last, h)
+        squares(last, 0, SIZES[last])
         quantise(last)
         multiply(last)
         finish(last - 1)

@@ -132,7 +132,7 @@ def tile_proto_metric_t_kernel(tc, x1, x2, out):
                 g_t = grp_pool.tile([P, SIZES[s] * D], BF16, name="grp", tag="grp", align_bytes=64)
                 grouped[s] = g_t
             dst = grouped[s][:].bitcast(F32)[:, h * 4 * P : (h + 1) * 4 * P]
-            if (h == 3 and s > 5) or (h == 2 and s == n_batches - 2) or s == n_batches - 1:
+            if (h == 3 and s > 5) or (h == 2 and s in (8, 12, 16, 17)) or s == n_batches - 1:
                 nc.scalar.copy(
                     out=dst.rearrange("p (a i u) -> p a i u", a=2, u=2),
                     in_=banks[s][h][:].rearrange("p (a u i) -> p a i u", a=2, u=2),
@@ -195,6 +195,12 @@ def tile_proto_metric_t_kernel(tc, x1, x2, out):
                     accum_out=q_sq[s][:, a : a + 1],
                 )
 
+        def store(s, o_t, a0, a1):
+            rows = out[first[s] * P : (first[s] + SIZES[s]) * P, :].rearrange("(p t) j -> p t j", t=SIZES[s])
+            nc.sync.dma_start(
+                out=rows[:, a0:a1, :], in_=o_t[:, a0 * N : a1 * N].rearrange("p (t j) -> p t j", j=N)
+            )
+
         def finish(s):
             t = SIZES[s]
             o_t = o_pool.tile([P, t * N], F32, name="o", tag="o")
@@ -208,8 +214,9 @@ def tile_proto_metric_t_kernel(tc, x1, x2, out):
                     op0=ALU.subtract,
                     op1=ALU.subtract,
                 )
-            rows = out[first[s] * P : (first[s] + t) * P, :]
-            nc.sync.dma_start(out=rows.rearrange("(p t) j -> p (t j)", t=t), in_=o_t[:])
+                if s == n_batches - 1 and a == t // 2 - 1:
+                    store(s, o_t, 0, t // 2)
+            store(s, o_t, t // 2 if s == n_batches - 1 else 0, t)
             if loaded[0] < n_batches:
                 load(loaded[0])
 

from contextlib import ExitStack

import concourse.mybir as mybir
from concourse.masks import make_identity

F32 = mybir.dt.float32
BF16 = mybir.dt.bfloat16
U32 = mybir.dt.uint32
U8 = mybir.dt.uint8
FP8X4 = mybir.dt.float8_e4m3fn_x4
ALU = mybir.AluOpType
ACT = mybir.ActivationFunctionType

P = 128
B = 16384
N = 128
SHOT = 5
D = 512
W = D // 2
FLOPS = 2 * B * N * D

SIZES = (2, 2, 4, 4) + (8,) * 14 + (4,)
GRAM = range(5, 17)
assert sum(SIZES) * P == B
FIRST_LOADS = 9


def tile_proto_metric_t_kernel(tc, x1, x2, out):
    nc = tc.nc
    q_rows = x1.rearrange("b d x y -> b (d x y)")
    shots = x2.rearrange("n s d x y -> n (s d x y)")
    n_batches = len(SIZES)
    first = [sum(SIZES[:s]) for s in range(n_batches)]

    with ExitStack() as ctx:
        const = ctx.enter_context(tc.tile_pool(name="const", bufs=1))
        grp_pool = ctx.enter_context(tc.tile_pool(name="grp", bufs=3))
        code_pool = ctx.enter_context(tc.tile_pool(name="code", bufs=6))
        junk_pool = ctx.enter_context(tc.tile_pool(name="junk", bufs=4))
        o_pool = ctx.enter_context(tc.tile_pool(name="o", bufs=4))
        ps_t = ctx.enter_context(tc.psum_pool(name="ps_t", bufs=4))
        ps_m = ctx.enter_context(tc.psum_pool(name="ps_m", bufs=3))
        ps_j = ctx.enter_context(tc.psum_pool(name="ps_j", bufs=1))
        sq_pool = ctx.enter_context(tc.tile_pool(name="sq", bufs=4))
        ctx.enter_context(tc.manual_schedule())

        x_sb = {}
        banks = {}
        grouped = {}
        codes = {}
        planes = {}
        q_sq = {}
        cross = {}
        sums_g = {}
        q_sq_g = {}
        loaded = [0]

        def g_tiles(s):
            return 1 if s in GRAM else 0

        def g_squares(s):
            sums_g[s] = []
            for a in range(g_tiles(s)):
                sq = sq_pool.tile([P, D], F32, name="sq", tag="sq")
                half = sq_pool.tile([P, D // 2], F32, name="half", tag="half")
                quarter = sq_pool.tile([P, D // 4], F32, name="quarter", tag="quarter")
                x_t = grouped[s][:, a * D : (a + 1) * D]
                nc.gpsimd.tensor_tensor(out=sq[:], in0=x_t, in1=x_t, op=ALU.mult)
                v4 = sq[:].rearrange("p (i t) -> p i t", t=4)
                nc.gpsimd.tensor_tensor(
                    out=half[:].rearrange("p (i t) -> p i t", t=2), in0=v4[:, :, 0:2], in1=v4[:, :, 2:4], op=ALU.add
                )
                v2 = half[:].rearrange("p (i t) -> p i t", t=2)
                nc.gpsimd.tensor_tensor(out=quarter[:], in0=v2[:, :, 0], in1=v2[:, :, 1], op=ALU.add)
                sums_g[s].append(quarter)

        def gram_tile(s):
            return g_tiles(s) if s in GRAM else None

        def gram_diagonal(s):
            junk = junk_pool.tile([P, N], F32, name="junk_g", tag="junk_g")
            a = gram_tile(s)
            nc.vector.scalar_tensor_tensor(
                out=junk[:],
                in0=q_sq_g[s][:, 0:P],
                scalar=1.0,
                in1=ident_f[:],
                op0=ALU.mult,
                op1=ALU.mult,
                accum_out=q_sq[s][:, a : a + 1],
            )

        def g_sum(s):
            cols = ps_j.tile([P, 4 * N], F32, name="cols", tag="cols")
            if s in GRAM:
                a = gram_tile(s)
                g4 = grouped[s][:, a * D : (a + 1) * D].rearrange("p (i t) -> p t i", t=4)
                for k in range(4):
                    nc.tensor.matmul(
                        out=cols[:, 0:P], lhsT=g4[:, k, :], rhs=g4[:, k, :], start=(k == 0), stop=(k == 3)
                    )
            for a in range(g_tiles(s)):
                nc.tensor.matmul(
                    out=cols[:, P + a : P + a + 1], lhsT=sums_g[s][a][:], rhs=ones[:, 0:1], start=True, stop=True
                )
            q_sq_g[s] = cols

        def load(s):
            t = SIZES[s]
            x_t = const.tile([P, t * D], BF16, name="x%d" % s)
            rows = q_rows[first[s] * P : (first[s] + t) * P, :]
            nc.sync.dma_start(out=x_t[:], in_=rows.rearrange("(p t) d -> p (t d)", t=t))
            x_sb[s] = x_t
            loaded[0] = s + 1

        def transposes(s, h0=0, h1=None):
            words = x_sb[s][:].bitcast(F32)
            if h0 == 0:
                banks[s] = []
            for h in range(h0, SIZES[s] // 2 if h1 is None else h1):
                bank = ps_t.tile([P, 4 * P], F32, name="xt", tag="xt")
                for k in range(4):
                    nc.tensor.transpose(
                        out=bank[:, k * P : (k + 1) * P],
                        in_=words[:, (4 * h + k) * P : (4 * h + k + 1) * P],
                        identity=ident_f[:],
                    )
                banks[s].append(bank)

        def evacuate(s, h):
            if h == 0:
                g_t = grp_pool.tile([P, SIZES[s] * D], BF16, name="grp", tag="grp", align_bytes=64)
                grouped[s] = g_t
            dst = grouped[s][:].bitcast(F32)[:, h * 4 * P : (h + 1) * 4 * P]
            if (h == 3 and s > 5) or (h == 2 and s in (8, 12, 16, 17)) or s == n_batches - 1:
                nc.scalar.copy(
                    out=dst.rearrange("p (a i u) -> p a i u", a=2, u=2),
                    in_=banks[s][h][:].rearrange("p (a u i) -> p a i u", a=2, u=2),
                )
            else:
                nc.vector.tensor_copy(
                    out=dst.rearrange("p (a i u) -> p a i u", a=2, u=2),
                    in_=banks[s][h][:].rearrange("p (a u i) -> p a i u", a=2, u=2),
                )

        def quantise(s):
            c_t = code_pool.tile([P, SIZES[s] * P], U32, name="codes", tag="codes", align_bytes=64)
            s_t = code_pool.tile([P, SIZES[s] * P], U8, name="plane", tag="plane", align_bytes=64)
            nc.vector.quantize_mx(out=c_t[:].bitcast(FP8X4), scales=s_t[:], in_=grouped[s][:])
            codes[s] = c_t
            planes[s] = s_t

        def keep_warm(s, passes):
            if s not in cross:
                acc = ps_m.tile([P, 4 * N], F32, name="acc", tag="acc")
                cross[s] = [acc]
            for b in range(passes):
                nc.tensor.matmul_mx(
                    out=cross[s][0][:],
                    lhsT=p_codes[:].bitcast(FP8X4),
                    lhsT_scale=p_plane[:],
                    rhs=codes[s - 1][:, 0 : 4 * P].bitcast(FP8X4),
                    rhs_scale=planes[s - 1][:, 0 : 4 * P],
                    start=True,
                    stop=True,
                )

        def multiply(s):
            if s not in cross:
                cross[s] = []
            for a in range(SIZES[s]):
                if a % 4 == 0 and len(cross[s]) <= a // 4:
                    acc = ps_m.tile([P, 4 * N], F32, name="acc", tag="acc")
                    cross[s].append(acc)
                nc.tensor.matmul_mx(
                    out=cross[s][a // 4][:, (a % 4) * N : (a % 4 + 1) * N],
                    lhsT=codes[s][:, a * P : (a + 1) * P].bitcast(FP8X4),
                    lhsT_scale=planes[s][:, a * P : (a + 1) * P],
                    rhs=p_codes[:].bitcast(FP8X4),
                    rhs_scale=p_plane[:],
                    start=True,
                    stop=True,
                )

        def squares(s, a0, a1):
            if s not in q_sq:
                n_t = const.tile([P, SIZES[s]], F32, name="qsq%d" % s)
                q_sq[s] = n_t
            for a in range(a0, a1):
                junk = junk_pool.tile([P, D], BF16, name="junk", tag="junk")
                nc.scalar.activation(
                    out=junk[:],
                    in_=x_sb[s][:, a * D : (a + 1) * D],
                    func=ACT.Square,
                    accum_out=q_sq[s][:, a : a + 1],
                )

        def store(s, o_t, a0, a1):
            rows = out[first[s] * P : (first[s] + SIZES[s]) * P, :].rearrange("(p t) j -> p t j", t=SIZES[s])
            nc.sync.dma_start(
                out=rows[:, a0:a1, :], in_=o_t[:, a0 * N : a1 * N].rearrange("p (t j) -> p t j", j=N)
            )

        def finish(s):
            t = SIZES[s]
            o_t = o_pool.tile([P, t * N], F32, name="o", tag="o")
            g = g_tiles(s)
            for a in ([2, 0, 1] + list(range(3, t)) if g else range(t)):
                nc.vector.scalar_tensor_tensor(
                    out=o_t[:, a * N : (a + 1) * N],
                    in0=cross[s][a // 4][:, (a % 4) * N : (a % 4 + 1) * N],
                    scalar=(q_sq_g[s][:, P + a : P + a + 1] if a < g else q_sq[s][:, a : a + 1]),
                    in1=p_sq[:],
                    op0=ALU.subtract,
                    op1=ALU.subtract,
                )
                if s == n_batches - 1 and a == t // 2 - 1:
                    store(s, o_t, 0, t // 2)
            store(s, o_t, t // 2 if s == n_batches - 1 else 0, t)
            if loaded[0] < n_batches:
                load(loaded[0])

        for s in range(4):
            load(s)
        x2_sb = const.tile([P, SHOT * D], BF16, name="x2_sb")
        nc.sync.dma_start(out=x2_sb[:], in_=shots)
        for s in range(4, FIRST_LOADS):
            load(s)
        ident_f = const.tile([P, P], F32, name="ident_f")
        make_identity(nc, ident_f[:])
        ones = const.tile([P, P], F32, name="ones")
        nc.vector.memset(ones[:], 1.0)

        x2_sum = const.tile([P, D], F32, name="x2_sum")
        nc.gpsimd.tensor_tensor(out=x2_sum[:], in0=x2_sb[:, 0:D], in1=x2_sb[:, D : 2 * D], op=ALU.add)
        for s in range(2, SHOT):
            nc.gpsimd.tensor_tensor(
                out=x2_sum[:], in0=x2_sum[:], in1=x2_sb[:, s * D : (s + 1) * D], op=ALU.add
            )

        transposes(0)
        squares(0, 0, 2)
        evacuate(0, 0)
        transposes(1)
        squares(1, 0, 2)
        evacuate(1, 0)
        quantise(0)
        transposes(2)
        squares(2, 0, 4)
        quantise(1)
        evacuate(2, 0)
        evacuate(2, 1)
        transposes(3)
        squares(3, 0, 4)
        quantise(2)
        evacuate(3, 0)
        evacuate(3, 1)
        transposes(4)
        quantise(3)
        for h in range(4):
            evacuate(4, h)
        squares(4, 0, 5)
        transposes(5)

        sums = ps_m.tile([P, 4 * N], F32, name="sums", tag="acc")
        for t4 in range(4):
            c0 = 256 * (t4 // 2)
            nc.tensor.transpose(
                out=sums[:, t4 * N : (t4 + 1) * N],
                in_=x2_sum[:, c0 + t4 % 2 : c0 + 256 : 2],
                identity=ident_f[:],
            )
        p_junk = const.tile([P, D], BF16, name="p_junk")
        p_norm = const.tile([P, 1], F32, name="p_norm")
        nc.scalar.activation(
            out=p_junk[:], in_=x2_sum[:], func=ACT.Square, scale=1.0 / SHOT, accum_out=p_norm[:]
        )
        for h in range(4):
            evacuate(5, h)
            if h == 0:
                g_squares(5)
        squares(4, 5, 8)
        norms = ps_m.tile([P, N], F32, name="norms", tag="acc")
        nc.tensor.matmul(
            out=norms[:], lhsT=p_norm[:].to_broadcast([P, P]), rhs=ident_f[:], start=True, stop=True
        )
        transposes(6)
        p_grp = const.tile([P, 4 * N], BF16, name="p_grp", align_bytes=64)
        nc.vector.tensor_scalar_mul(
            out=p_grp[:].rearrange("p (n t) -> p n t", t=4),
            in0=sums[:].rearrange("p (t n) -> p n t", t=4),
            scalar1=2.0 / SHOT,
        )
        quantise(4)
        p_codes = const.tile([P, N], U32, name="p_codes", align_bytes=64)
        p_plane = const.tile([P, N], U8, name="p_plane", align_bytes=64)
        nc.vector.quantize_mx(out=p_codes[:].bitcast(FP8X4), scales=p_plane[:], in_=p_grp[:])
        quantise(5)
        p_sq = const.tile([P, N], F32, name="p_sq")
        nc.vector.tensor_copy(out=p_sq[:], in_=norms[:])
        for s in (5, 6):
            squares(s, g_tiles(s) + (s in GRAM), SIZES[s])
        multiply(0)
        multiply(1)
        multiply(2)
        finish(0)
        multiply(3)
        finish(1)
        finish(2)
        multiply(4)
        finish(3)
        g_sum(5)
        multiply(5)
        finish(4)

        last = n_batches - 1
        for s in range(6, last):
            for h in range(SIZES[s] // 2):
                evacuate(s, h)
                if h == 0:
                    g_squares(s)
            half = SIZES[s + 1] // 4
            transposes(s + 1, 0, half)
            keep_warm(s, 2)
            transposes(s + 1, half, None)
            keep_warm(s, 1)
            if g_tiles(s):
                g_sum(s)
            if s < last - 1:
                squares(s + 1, g_tiles(s + 1) + (s + 1 in GRAM), SIZES[s + 1])
            if s - 1 in GRAM:
                gram_diagonal(s - 1)
            finish(s - 1)
            quantise(s)
            multiply(s)
        for h in range(SIZES[last] // 2):
            evacuate(last, h)
        squares(last, 0, SIZES[last])
        quantise(last)
        multiply(last)
        finish(last - 1)
        finish(last)
